import numpy as np
import ml_dtypes

BF16 = ml_dtypes.bfloat16


def bf(x):
    return np.asarray(x, np.float32).astype(BF16)


def f32(x):
    return np.asarray(x, np.float32)


def f64(x):
    return np.asarray(x).astype(np.float64)


def striped(idx):
    return np.tile(idx.reshape(-1, 16).T, (8, 1))


H, D, C, S, N, T, BQ, L, NQ = 8, 128, 1024, 4096, 2048, 4, 256, 512, 1024
SM_SCALE = 0.125


def setup_inputs():
    return {"q": bf(np.random.standard_normal((C, NQ))), "k": f32(np.random.standard_normal((C, S))), "v": bf(np.random.standard_normal((C, N))), "offs": striped(np.random.permutation(S)[:N])}


def reference(q, k, v, offs):
    idx = offs[:16].T.reshape(-1)
    kp = f64(k)[:, idx].reshape(H, D, T, L)
    qb = f64(q).reshape(H, D, T, BQ)
    vb = f64(v).reshape(H, D, T, L)
    s = SM_SCALE * np.matmul(qb.transpose(0, 2, 3, 1), kp.transpose(0, 2, 1, 3))
    e = np.exp(s - s.max(axis=-1, keepdims=True))
    p = e / e.sum(axis=-1, keepdims=True)
    o = np.matmul(vb.transpose(0, 2, 1, 3), p.transpose(0, 1, 3, 2))
    return o.transpose(0, 2, 1, 3).reshape(C, NQ)

@@ -1,0 +1,97 @@
+import concourse.mybir as mybir
+from concourse.masks import make_identity
+
+F32 = mybir.dt.float32
+BF16 = mybir.dt.bfloat16
+U16 = mybir.dt.uint16
+COPY = mybir.ActivationFunctionType.Copy
+EXP = mybir.ActivationFunctionType.Exp
+MULT = mybir.AluOpType.mult
+MAX = mybir.AluOpType.max
+AXIS_X = mybir.AxisListType.X
+
+P = 128
+HEADS = 8
+STORE = 4096
+LIST = 2048
+BLOCKS = 4
+BQ = 256
+BK = 512
+NQ = BLOCKS * BQ
+SM_SCALE = 0.125
+
+FLOPS = 2 * 2 * HEADS * BLOCKS * BQ * BK * P
+
+
+def tile_sparseattention_b_kernel(tc, q, k, v, offs, out):
+    nc = tc.nc
+    with (
+        tc.tile_pool(name="held", bufs=1) as held,
+        tc.tile_pool(name="store", bufs=4) as store,
+        tc.tile_pool(name="heads", bufs=2) as heads,
+        tc.tile_pool(name="work", bufs=3) as work,
+        tc.tile_pool(name="stats", bufs=6) as stats,
+        tc.psum_pool(name="scores", bufs=3) as scores,
+        tc.psum_pool(name="flipped", bufs=3) as flipped,
+        tc.psum_pool(name="products", bufs=2) as products,
+    ):
+        offsets = held.tile([P, LIST // 16], U16, name="offsets")
+        nc.sync.dma_start(offsets[:], offs)
+        ident = held.tile([P, P], BF16, name="ident")
+        make_identity(nc, ident[:])
+
+        for h in range(HEADS):
+            rows = slice(h * P, (h + 1) * P)
+            k_win = store.tile([P, STORE], F32, name="k_win")
+            nc.sync.dma_start(k_win[:], k[rows, :])
+            v_sb = heads.tile([P, LIST], BF16, name="v_sb")
+            nc.sync.dma_start(v_sb[:], v[rows, :])
+            q_sb = heads.tile([P, NQ], BF16, name="q_sb")
+            nc.sync.dma_start(q_sb[:], q[rows, :])
+
+            v_t = heads.tile([P, LIST // P, P], BF16, name="v_t")
+            for g in range(2):
+                vt_ps = flipped.tile([P, 8, P], BF16, name="vt_ps", tag="flip")
+                for b in range(8):
+                    j0 = (g * 8 + b) * P
+                    nc.tensor.transpose(vt_ps[:, b, :], v_sb[:, j0 : j0 + P], ident[:])
+                nc.vector.tensor_copy(v_t[:, g * 8 : (g + 1) * 8, :], vt_ps[:])
+
+            keys = heads.tile([P, LIST], BF16, name="keys")
+            for t in range(BLOCKS):
+                picked = work.tile([P, BK], F32, name="picked")
+                piece = offsets[:, t * (BK // 16) : (t + 1) * (BK // 16)]
+                nc.scalar.activation(picked[:], k_win[:].indirect(piece), COPY)
+                block_keys = keys[:, t * BK : (t + 1) * BK]
+                nc.gpsimd.tensor_scalar(block_keys, picked[:], SM_SCALE, 1.0, MULT, MULT)
+
+                pt_ps = flipped.tile([P, BK // P, BQ], BF16, name="pt_ps", tag="flip")
+                for nb in range(BQ // P):
+                    n0 = t * BQ + nb * P
+                    s_ps = scores.tile([P, BK], F32, name="s_ps")
+                    nc.tensor.matmul(s_ps[:], q_sb[:, n0 : n0 + P], block_keys, start=True, stop=True)
+                    neg_max = stats.tile([P, 1], F32, name="neg_max")
+                    nc.vector.tensor_reduce(neg_max[:], s_ps[:], AXIS_X, MAX, negate=True)
+                    e_sb = work.tile([P, BK], F32, name="e_sb")
+                    e_sum = stats.tile([P, 1], F32, name="e_sum")
+                    nc.scalar.activation(e_sb[:], s_ps[:], EXP, bias=neg_max[:], accum_out=e_sum[:])
+                    r_sum = stats.tile([P, 1], F32, name="r_sum")
+                    nc.vector.reciprocal(r_sum[:], e_sum[:])
+                    p_sb = work.tile([P, BK], BF16, name="p_sb")
+                    nc.gpsimd.tensor_scalar(p_sb[:], e_sb[:], r_sum[:], 1.0, MULT, MULT)
+                    for jb in range(BK // P):
+                        nc.tensor.transpose(
+                            pt_ps[:, jb, nb * P : (nb + 1) * P], p_sb[:, jb * P : (jb + 1) * P], ident[:]
+                        )
+                p_t = work.tile([P, BK // P, BQ], BF16, name="p_t")
+                nc.vector.tensor_copy(p_t[:], pt_ps[:])
+
+                o_ps = products.tile([P, BQ], F32, name="o_ps")
+                for jb in range(BK // P):
+                    nc.tensor.matmul(
+                        o_ps[:], v_t[:, t * (BK // P) + jb, :], p_t[:, jb, :],
+                        start=(jb == 0), stop=(jb == BK // P - 1),
+                    )
+                o_sb = work.tile([P, BQ], F32, name="o_sb")
+                nc.vector.tensor_copy(o_sb[:], o_ps[:])
+                nc.sync.dma_start(out[rows, t * BQ : (t + 1) * BQ], o_sb[:])

@@ -18,6 +18,9 @@ BLOCKS = 4
 BQ = 256
 BK = 512
 NQ = BLOCKS * BQ
+QB = BQ // P
+KB = BK // P
+UNITS = HEADS * BLOCKS
 SM_SCALE = 0.125
 
 FLOPS = 2 * 2 * HEADS * BLOCKS * BQ * BK * P
@@ -27,71 +30,102 @@ def tile_sparseattention_b_kernel(tc, q, k, v, offs, out):
     nc = tc.nc
     with (
         tc.tile_pool(name="held", bufs=1) as held,
-        tc.tile_pool(name="store", bufs=4) as store,
-        tc.tile_pool(name="heads", bufs=2) as heads,
-        tc.tile_pool(name="work", bufs=3) as work,
-        tc.tile_pool(name="stats", bufs=6) as stats,
-        tc.psum_pool(name="scores", bufs=3) as scores,
-        tc.psum_pool(name="flipped", bufs=3) as flipped,
-        tc.psum_pool(name="products", bufs=2) as products,
+        tc.tile_pool(name="store", bufs=3) as store,
+        tc.tile_pool(name="heads", bufs=3) as heads,
+        tc.tile_pool(name="work", bufs=6) as work,
+        tc.tile_pool(name="stats", bufs=12) as stats,
+        tc.psum_pool(name="scores", bufs=4) as scores,
+        tc.psum_pool(name="flipped_p", bufs=2) as flipped_p,
+        tc.psum_pool(name="flipped_v", bufs=1) as flipped_v,
+        tc.psum_pool(name="products", bufs=1) as products,
     ):
         offsets = held.tile([P, LIST // 16], U16, name="offsets")
         nc.sync.dma_start(offsets[:], offs)
         ident = held.tile([P, P], BF16, name="ident")
         make_identity(nc, ident[:])
+        warm = held.tile([P, 2], F32, name="warm")
+        nc.vector.memset(warm[:], 0.0)
+        nc.scalar.activation(warm[:, 1:2], warm[:, 0:1], EXP)
 
-        for h in range(HEADS):
+        k_win, q_sb, v_sb = {}, {}, {}
+        keys, v_t = {}, {}
+        s_ps, neg_max, p_sb = {}, {}, {}
+
+        def load_head(h):
             rows = slice(h * P, (h + 1) * P)
-            k_win = store.tile([P, STORE], F32, name="k_win")
-            nc.sync.dma_start(k_win[:], k[rows, :])
-            v_sb = heads.tile([P, LIST], BF16, name="v_sb")
-            nc.sync.dma_start(v_sb[:], v[rows, :])
-            q_sb = heads.tile([P, NQ], BF16, name="q_sb")
-            nc.sync.dma_start(q_sb[:], q[rows, :])
+            k_win[h] = store.tile([P, STORE], F32, name="k_win")
+            nc.sync.dma_start(k_win[h][:], k[rows, :])
+            q_sb[h] = heads.tile([P, NQ], BF16, name="q_sb")
+            nc.sync.dma_start(q_sb[h][:], q[rows, :])
+            v_sb[h] = heads.tile([P, LIST], BF16, name="v_sb")
+            nc.sync.dma_start(v_sb[h][:], v[rows, :])
 
-            v_t = heads.tile([P, LIST // P, P], BF16, name="v_t")
-            for g in range(2):
-                vt_ps = flipped.tile([P, 8, P], BF16, name="vt_ps", tag="flip")
-                for b in range(8):
-                    j0 = (g * 8 + b) * P
-                    nc.tensor.transpose(vt_ps[:, b, :], v_sb[:, j0 : j0 + P], ident[:])
-                nc.vector.tensor_copy(v_t[:, g * 8 : (g + 1) * 8, :], vt_ps[:])
+        def pick_keys(u):
+            h, t = divmod(u, BLOCKS)
+            if t == 0 and h + 1 < HEADS:
+                load_head(h + 1)
+            picked = work.tile([P, BK], F32, name="picked")
+            piece = offsets[:, t * (BK // 16) : (t + 1) * (BK // 16)]
+            nc.scalar.activation(picked[:], k_win[h][:].indirect(piece), COPY)
+            keys[u] = work.tile([P, BK], BF16, name="keys")
+            rounder = nc.vector if t % 2 == 0 else nc.gpsimd
+            rounder.tensor_scalar(keys[u][:], picked[:], SM_SCALE, 1.0, MULT, MULT)
 
-            keys = heads.tile([P, LIST], BF16, name="keys")
-            for t in range(BLOCKS):
-                picked = work.tile([P, BK], F32, name="picked")
-                piece = offsets[:, t * (BK // 16) : (t + 1) * (BK // 16)]
-                nc.scalar.activation(picked[:], k_win[:].indirect(piece), COPY)
-                block_keys = keys[:, t * BK : (t + 1) * BK]
-                nc.gpsimd.tensor_scalar(block_keys, picked[:], SM_SCALE, 1.0, MULT, MULT)
+        def score(u, nb):
+            h, t = divmod(u, BLOCKS)
+            n0 = t * BQ + nb * P
+            s_ps[u, nb] = scores.tile([P, BK], F32, name="s_ps")
+            nc.tensor.matmul(s_ps[u, nb][:], q_sb[h][:, n0 : n0 + P], keys[u][:], start=True, stop=True)
+            neg_max[u, nb] = stats.tile([P, 1], F32, name="neg_max")
+            nc.vector.tensor_reduce(neg_max[u, nb][:], s_ps[u, nb][:], AXIS_X, MAX, negate=True)
 
-                pt_ps = flipped.tile([P, BK // P, BQ], BF16, name="pt_ps", tag="flip")
-                for nb in range(BQ // P):
-                    n0 = t * BQ + nb * P
-                    s_ps = scores.tile([P, BK], F32, name="s_ps")
-                    nc.tensor.matmul(s_ps[:], q_sb[:, n0 : n0 + P], block_keys, start=True, stop=True)
-                    neg_max = stats.tile([P, 1], F32, name="neg_max")
-                    nc.vector.tensor_reduce(neg_max[:], s_ps[:], AXIS_X, MAX, negate=True)
-                    e_sb = work.tile([P, BK], F32, name="e_sb")
-                    e_sum = stats.tile([P, 1], F32, name="e_sum")
-                    nc.scalar.activation(e_sb[:], s_ps[:], EXP, bias=neg_max[:], accum_out=e_sum[:])
-                    r_sum = stats.tile([P, 1], F32, name="r_sum")
-                    nc.vector.reciprocal(r_sum[:], e_sum[:])
-                    p_sb = work.tile([P, BK], BF16, name="p_sb")
-                    nc.gpsimd.tensor_scalar(p_sb[:], e_sb[:], r_sum[:], 1.0, MULT, MULT)
-                    for jb in range(BK // P):
-                        nc.tensor.transpose(
-                            pt_ps[:, jb, nb * P : (nb + 1) * P], p_sb[:, jb * P : (jb + 1) * P], ident[:]
-                        )
-                p_t = work.tile([P, BK // P, BQ], BF16, name="p_t")
-                nc.vector.tensor_copy(p_t[:], pt_ps[:])
+        def flip_values(u):
+            h, t = divmod(u, BLOCKS)
+            vt_ps = flipped_v.tile([P, KB, P], BF16, name="vt_ps")
+            for jb in range(KB):
+                j0 = t * BK + jb * P
+                nc.tensor.transpose(vt_ps[:, jb, :], v_sb[h][:, j0 : j0 + P], ident[:])
+            v_t[u] = work.tile([P, KB, P], BF16, name="v_t")
+            nc.vector.tensor_copy(v_t[u][:], vt_ps[:])
 
-                o_ps = products.tile([P, BQ], F32, name="o_ps")
-                for jb in range(BK // P):
-                    nc.tensor.matmul(
-                        o_ps[:], v_t[:, t * (BK // P) + jb, :], p_t[:, jb, :],
-                        start=(jb == 0), stop=(jb == BK // P - 1),
+        def soften(u, nb):
+            e_sb = work.tile([P, BK], F32, name="e_sb")
+            e_sum = stats.tile([P, 1], F32, name="e_sum")
+            nc.scalar.activation(e_sb[:], s_ps[u, nb][:], EXP, bias=neg_max[u, nb][:], accum_out=e_sum[:])
+            r_sum = stats.tile([P, 1], F32, name="r_sum")
+            nc.vector.reciprocal(r_sum[:], e_sum[:])
+            p_sb[u, nb] = work.tile([P, BK], BF16, name="p_sb")
+            nc.gpsimd.tensor_scalar(p_sb[u, nb][:], e_sb[:], r_sum[:], 1.0, MULT, MULT)
+
+        def weigh(u):
+            h, t = divmod(u, BLOCKS)
+            pt_ps = flipped_p.tile([P, KB, BQ], BF16, name="pt_ps")
+            for nb in range(QB):
+                for jb in range(KB):
+                    nc.tensor.transpose(
+                        pt_ps[:, jb, nb * P : (nb + 1) * P], p_sb[u, nb][:, jb * P : (jb + 1) * P], ident[:]
                     )
-                o_sb = work.tile([P, BQ], F32, name="o_sb")
-                nc.vector.tensor_copy(o_sb[:], o_ps[:])
-                nc.sync.dma_start(out[rows, t * BQ : (t + 1) * BQ], o_sb[:])
+            p_t = work.tile([P, KB, BQ], BF16, name="p_t")
+            nc.vector.tensor_copy(p_t[:], pt_ps[:])
+            o_ps = products.tile([P, BQ], F32, name="o_ps")
+            for jb in range(KB):
+                nc.tensor.matmul(o_ps[:], v_t[u][:, jb, :], p_t[:, jb, :], start=(jb == 0), stop=(jb == KB - 1))
+            o_sb = work.tile([P, BQ], F32, name="o_sb")
+            nc.vector.tensor_copy(o_sb[:], o_ps[:])
+            nc.sync.dma_start(out[h * P : (h + 1) * P, t * BQ : (t + 1) * BQ], o_sb[:])
+
+        load_head(0)
+        for u in range(3):
+            pick_keys(u)
+        for u in range(2):
+            for nb in range(QB):
+                score(u, nb)
+        for i in range(UNITS):
+            if i + 3 < UNITS:
+                pick_keys(i + 3)
+            for nb in range(QB):
+                soften(i, nb)
+                if i + 2 < UNITS:
+                    score(i + 2, nb)
+            flip_values(i)
+            weigh(i)

@@ -48,7 +48,7 @@ def tile_sparseattention_b_kernel(tc, q, k, v, offs, out):
         nc.scalar.activation(warm[:, 1:2], warm[:, 0:1], EXP)
 
         k_win, q_sb, v_sb = {}, {}, {}
-        keys, v_t = {}, {}
+        keys, v_t, p_t = {}, {}, {}
         s_ps, neg_max, p_sb = {}, {}, {}
 
         def load_head(h):
@@ -97,19 +97,21 @@ def tile_sparseattention_b_kernel(tc, q, k, v, offs, out):
             p_sb[u, nb] = work.tile([P, BK], BF16, name="p_sb")
             nc.gpsimd.tensor_scalar(p_sb[u, nb][:], e_sb[:], r_sum[:], 1.0, MULT, MULT)
 
-        def weigh(u):
-            h, t = divmod(u, BLOCKS)
+        def flip_weights(u):
             pt_ps = flipped_p.tile([P, KB, BQ], BF16, name="pt_ps")
             for nb in range(QB):
                 for jb in range(KB):
                     nc.tensor.transpose(
                         pt_ps[:, jb, nb * P : (nb + 1) * P], p_sb[u, nb][:, jb * P : (jb + 1) * P], ident[:]
                     )
-            p_t = work.tile([P, KB, BQ], BF16, name="p_t")
-            nc.vector.tensor_copy(p_t[:], pt_ps[:])
+            p_t[u] = work.tile([P, KB, BQ], BF16, name="p_t")
+            nc.vector.tensor_copy(p_t[u][:], pt_ps[:])
+
+        def weigh(u):
+            h, t = divmod(u, BLOCKS)
             o_ps = products.tile([P, BQ], F32, name="o_ps")
             for jb in range(KB):
-                nc.tensor.matmul(o_ps[:], v_t[u][:, jb, :], p_t[:, jb, :], start=(jb == 0), stop=(jb == KB - 1))
+                nc.tensor.matmul(o_ps[:], v_t[u][:, jb, :], p_t[u][:, jb, :], start=(jb == 0), stop=(jb == KB - 1))
             o_sb = work.tile([P, BQ], F32, name="o_sb")
             nc.vector.tensor_copy(o_sb[:], o_ps[:])
             nc.sync.dma_start(out[h * P : (h + 1) * P, t * BQ : (t + 1) * BQ], o_sb[:])
@@ -120,12 +122,16 @@ def tile_sparseattention_b_kernel(tc, q, k, v, offs, out):
         for u in range(2):
             for nb in range(QB):
                 score(u, nb)
-        for i in range(UNITS):
+        for i in range(UNITS + 2):
+            if 0 <= i - 2:
+                weigh(i - 2)
+            if 0 <= i - 1 < UNITS:
+                flip_weights(i - 1)
             if i + 3 < UNITS:
                 pick_keys(i + 3)
-            for nb in range(QB):
-                soften(i, nb)
-                if i + 2 < UNITS:
-                    score(i + 2, nb)
-            flip_values(i)
-            weigh(i)
+            if i < UNITS:
+                for nb in range(QB):
+                    soften(i, nb)
+                    if i + 2 < UNITS:
+                        score(i + 2, nb)
+                flip_values(i)

@@ -86,7 +86,7 @@ def tile_sparseattention_b_kernel(tc, q, k, v, offs, out):
                 j0 = t * BK + jb * P
                 nc.tensor.transpose(vt_ps[:, jb, :], v_sb[h][:, j0 : j0 + P], ident[:])
             v_t[u] = work.tile([P, KB, P], BF16, name="v_t")
-            nc.vector.tensor_copy(v_t[u][:], vt_ps[:])
+            nc.scalar.copy(v_t[u][:], vt_ps[:])
 
         def soften(u, nb):
             e_sb = work.tile([P, BK], F32, name="e_sb")

@@ -86,7 +86,10 @@ def tile_sparseattention_b_kernel(tc, q, k, v, offs, out):
                 j0 = t * BK + jb * P
                 nc.tensor.transpose(vt_ps[:, jb, :], v_sb[h][:, j0 : j0 + P], ident[:])
             v_t[u] = work.tile([P, KB, P], BF16, name="v_t")
-            nc.scalar.copy(v_t[u][:], vt_ps[:])
+            if u % 2 == 0:
+                nc.scalar.copy(v_t[u][:], vt_ps[:])
+            else:
+                nc.vector.tensor_copy(v_t[u][:], vt_ps[:])
 
         def soften(u, nb):
             e_sb = work.tile([P, BK], F32, name="e_sb")

@@ -21,6 +21,7 @@ NQ = BLOCKS * BQ
 QB = BQ // P
 KB = BK // P
 UNITS = HEADS * BLOCKS
+PAIR = 2
 SM_SCALE = 0.125
 
 FLOPS = 2 * 2 * HEADS * BLOCKS * BQ * BK * P
@@ -48,7 +49,8 @@ def tile_sparseattention_b_kernel(tc, q, k, v, offs, out):
         nc.scalar.activation(warm[:, 1:2], warm[:, 0:1], EXP)
 
         k_win, q_sb, v_sb = {}, {}, {}
-        keys, v_t, p_t = {}, {}, {}
+        keys, p_t = {}, {}
+        v_t, o_ps = {}, {}
         s_ps, neg_max, p_sb = {}, {}, {}
 
         def load_head(h):
@@ -79,17 +81,17 @@ def tile_sparseattention_b_kernel(tc, q, k, v, offs, out):
             neg_max[u, nb] = stats.tile([P, 1], F32, name="neg_max")
             nc.vector.tensor_reduce(neg_max[u, nb][:], s_ps[u, nb][:], AXIS_X, MAX, negate=True)
 
-        def flip_values(u):
-            h, t = divmod(u, BLOCKS)
-            vt_ps = flipped_v.tile([P, KB, P], BF16, name="vt_ps")
-            for jb in range(KB):
+        def flip_values(w):
+            h, t = divmod(PAIR * w, BLOCKS)
+            vt_ps = flipped_v.tile([P, PAIR * KB, P], BF16, name="vt_ps")
+            for jb in range(PAIR * KB):
                 j0 = t * BK + jb * P
                 nc.tensor.transpose(vt_ps[:, jb, :], v_sb[h][:, j0 : j0 + P], ident[:])
-            v_t[u] = work.tile([P, KB, P], BF16, name="v_t")
-            if u % 2 == 0:
-                nc.scalar.copy(v_t[u][:], vt_ps[:])
+            v_t[w] = work.tile([P, PAIR * KB, P], BF16, name="v_t")
+            if w % 2 == 0:
+                nc.vector.tensor_copy(v_t[w][:], vt_ps[:])
             else:
-                nc.vector.tensor_copy(v_t[u][:], vt_ps[:])
+                nc.scalar.copy(v_t[w][:], vt_ps[:])
 
         def soften(u, nb):
             e_sb = work.tile([P, BK], F32, name="e_sb")
@@ -111,13 +113,22 @@ def tile_sparseattention_b_kernel(tc, q, k, v, offs, out):
             nc.vector.tensor_copy(p_t[u][:], pt_ps[:])
 
         def weigh(u):
-            h, t = divmod(u, BLOCKS)
-            o_ps = products.tile([P, BQ], F32, name="o_ps")
+            w, half = divmod(u, PAIR)
+            if half == 0:
+                o_ps[w] = products.tile([P, PAIR * BQ], F32, name="o_ps")
             for jb in range(KB):
-                nc.tensor.matmul(o_ps[:], v_t[u][:, jb, :], p_t[u][:, jb, :], start=(jb == 0), stop=(jb == KB - 1))
-            o_sb = work.tile([P, BQ], F32, name="o_sb")
-            nc.vector.tensor_copy(o_sb[:], o_ps[:])
-            nc.sync.dma_start(out[h * P : (h + 1) * P, t * BQ : (t + 1) * BQ], o_sb[:])
+                nc.tensor.matmul(
+                    o_ps[w][:, half * BQ : (half + 1) * BQ],
+                    v_t[w][:, half * KB + jb, :],
+                    p_t[u][:, jb, :],
+                    start=(jb == 0),
+                    stop=(jb == KB - 1),
+                )
+            if half == PAIR - 1:
+                h, t = divmod(PAIR * w, BLOCKS)
+                o_sb = work.tile([P, PAIR * BQ], F32, name="o_sb")
+                nc.vector.tensor_copy(o_sb[:], o_ps[w][:])
+                nc.sync.dma_start(out[h * P : (h + 1) * P, t * BQ : (t + PAIR) * BQ], o_sb[:])
 
         load_head(0)
         for u in range(3):
@@ -137,4 +148,5 @@ def tile_sparseattention_b_kernel(tc, q, k, v, offs, out):
                     soften(i, nb)
                     if i + 2 < UNITS:
                         score(i + 2, nb)
-                flip_values(i)
+                if i % PAIR == 0:
+                    flip_values(i // PAIR)

@@ -53,6 +53,9 @@ def tile_sparseattention_b_kernel(tc, q, k, v, offs, out):
         v_t, o_ps = {}, {}
         s_ps, neg_max, p_sb = {}, {}, {}
 
+        def flip(flipped, tile):
+            nc.tensor.matmul(flipped, tile, ident[:], start=True, stop=True)
+
         def load_head(h):
             rows = slice(h * P, (h + 1) * P)
             k_win[h] = store.tile([P, STORE], F32, name="k_win")
@@ -86,7 +89,7 @@ def tile_sparseattention_b_kernel(tc, q, k, v, offs, out):
             vt_ps = flipped_v.tile([P, PAIR * KB, P], BF16, name="vt_ps")
             for jb in range(PAIR * KB):
                 j0 = t * BK + jb * P
-                nc.tensor.transpose(vt_ps[:, jb, :], v_sb[h][:, j0 : j0 + P], ident[:])
+                flip(vt_ps[:, jb, :], v_sb[h][:, j0 : j0 + P])
             v_t[w] = work.tile([P, PAIR * KB, P], BF16, name="v_t")
             if w % 2 == 0:
                 nc.vector.tensor_copy(v_t[w][:], vt_ps[:])
@@ -106,9 +109,7 @@ def tile_sparseattention_b_kernel(tc, q, k, v, offs, out):
             pt_ps = flipped_p.tile([P, KB, BQ], BF16, name="pt_ps")
             for nb in range(QB):
                 for jb in range(KB):
-                    nc.tensor.transpose(
-                        pt_ps[:, jb, nb * P : (nb + 1) * P], p_sb[u, nb][:, jb * P : (jb + 1) * P], ident[:]
-                    )
+                    flip(pt_ps[:, jb, nb * P : (nb + 1) * P], p_sb[u, nb][:, jb * P : (jb + 1) * P])
             p_t[u] = work.tile([P, KB, BQ], BF16, name="p_t")
             nc.vector.tensor_copy(p_t[u][:], pt_ps[:])
 

@@ -53,9 +53,6 @@ def tile_sparseattention_b_kernel(tc, q, k, v, offs, out):
         v_t, o_ps = {}, {}
         s_ps, neg_max, p_sb = {}, {}, {}
 
-        def flip(flipped, tile):
-            nc.tensor.matmul(flipped, tile, ident[:], start=True, stop=True)
-
         def load_head(h):
             rows = slice(h * P, (h + 1) * P)
             k_win[h] = store.tile([P, STORE], F32, name="k_win")
@@ -89,12 +86,9 @@ def tile_sparseattention_b_kernel(tc, q, k, v, offs, out):
             vt_ps = flipped_v.tile([P, PAIR * KB, P], BF16, name="vt_ps")
             for jb in range(PAIR * KB):
                 j0 = t * BK + jb * P
-                flip(vt_ps[:, jb, :], v_sb[h][:, j0 : j0 + P])
+                nc.tensor.transpose(vt_ps[:, jb, :], v_sb[h][:, j0 : j0 + P], ident[:])
             v_t[w] = work.tile([P, PAIR * KB, P], BF16, name="v_t")
-            if w % 2 == 0:
-                nc.vector.tensor_copy(v_t[w][:], vt_ps[:])
-            else:
-                nc.scalar.copy(v_t[w][:], vt_ps[:])
+            nc.vector.tensor_copy(v_t[w][:], vt_ps[:])
 
         def soften(u, nb):
             e_sb = work.tile([P, BK], F32, name="e_sb")
@@ -109,7 +103,13 @@ def tile_sparseattention_b_kernel(tc, q, k, v, offs, out):
             pt_ps = flipped_p.tile([P, KB, BQ], BF16, name="pt_ps")
             for nb in range(QB):
                 for jb in range(KB):
-                    flip(pt_ps[:, jb, nb * P : (nb + 1) * P], p_sb[u, nb][:, jb * P : (jb + 1) * P])
+                    nc.tensor.matmul(
+                        pt_ps[:, jb, nb * P : (nb + 1) * P],
+                        p_sb[u, nb][:, jb * P : (jb + 1) * P],
+                        ident[:],
+                        start=True,
+                        stop=True,
+                    )
             p_t[u] = work.tile([P, KB, BQ], BF16, name="p_t")
             nc.vector.tensor_copy(p_t[u][:], pt_ps[:])
 
@@ -128,7 +128,10 @@ def tile_sparseattention_b_kernel(tc, q, k, v, offs, out):
             if half == PAIR - 1:
                 h, t = divmod(PAIR * w, BLOCKS)
                 o_sb = work.tile([P, PAIR * BQ], F32, name="o_sb")
-                nc.vector.tensor_copy(o_sb[:], o_ps[w][:])
+                if w % 2 == 0:
+                    nc.vector.tensor_copy(o_sb[:], o_ps[w][:])
+                else:
+                    nc.scalar.copy(o_sb[:], o_ps[w][:])
                 nc.sync.dma_start(out[h * P : (h + 1) * P, t * BQ : (t + PAIR) * BQ], o_sb[:])
 
         load_head(0)

@@ -33,8 +33,8 @@ def tile_sparseattention_b_kernel(tc, q, k, v, offs, out):
         tc.tile_pool(name="held", bufs=1) as held,
         tc.tile_pool(name="store", bufs=3) as store,
         tc.tile_pool(name="heads", bufs=3) as heads,
-        tc.tile_pool(name="work", bufs=6) as work,
-        tc.tile_pool(name="stats", bufs=12) as stats,
+        tc.tile_pool(name="work", bufs=12) as work,
+        tc.tile_pool(name="stats", bufs=24) as stats,
         tc.psum_pool(name="scores", bufs=4) as scores,
         tc.psum_pool(name="flipped_p", bufs=2) as flipped_p,
         tc.psum_pool(name="flipped_v", bufs=1) as flipped_v,

@@ -140,11 +140,11 @@ def tile_sparseattention_b_kernel(tc, q, k, v, offs, out):
         for u in range(2):
             for nb in range(QB):
                 score(u, nb)
-        for i in range(UNITS + 2):
-            if 0 <= i - 2:
-                weigh(i - 2)
-            if 0 <= i - 1 < UNITS:
-                flip_weights(i - 1)
+        for i in range(UNITS + 3):
+            if 0 <= i - 3:
+                weigh(i - 3)
+            if 0 <= i - 2 < UNITS:
+                flip_weights(i - 2)
             if i + 3 < UNITS:
                 pick_keys(i + 3)
             if i < UNITS:

@@ -36,9 +36,8 @@ def tile_sparseattention_b_kernel(tc, q, k, v, offs, out):
         tc.tile_pool(name="work", bufs=12) as work,
         tc.tile_pool(name="stats", bufs=24) as stats,
         tc.psum_pool(name="scores", bufs=4) as scores,
-        tc.psum_pool(name="flipped_p", bufs=2) as flipped_p,
-        tc.psum_pool(name="flipped_v", bufs=1) as flipped_v,
-        tc.psum_pool(name="products", bufs=1) as products,
+        tc.psum_pool(name="flipped", bufs=2) as flipped,
+        tc.psum_pool(name="products", bufs=2) as products,
     ):
         offsets = held.tile([P, LIST // 16], U16, name="offsets")
         nc.sync.dma_start(offsets[:], offs)
@@ -83,7 +82,7 @@ def tile_sparseattention_b_kernel(tc, q, k, v, offs, out):
 
         def flip_values(w):
             h, t = divmod(PAIR * w, BLOCKS)
-            vt_ps = flipped_v.tile([P, PAIR * KB, P], BF16, name="vt_ps")
+            vt_ps = flipped.tile([P, PAIR * KB, P], BF16, name="vt_ps", tag="flipped")
             for jb in range(PAIR * KB):
                 j0 = t * BK + jb * P
                 nc.tensor.transpose(vt_ps[:, jb, :], v_sb[h][:, j0 : j0 + P], ident[:])
@@ -100,7 +99,7 @@ def tile_sparseattention_b_kernel(tc, q, k, v, offs, out):
             nc.gpsimd.tensor_scalar(p_sb[u, nb][:], e_sb[:], r_sum[:], 1.0, MULT, MULT)
 
         def flip_weights(u):
-            pt_ps = flipped_p.tile([P, KB, BQ], BF16, name="pt_ps")
+            pt_ps = flipped.tile([P, KB, BQ], BF16, name="pt_ps", tag="flipped")
             for nb in range(QB):
                 for jb in range(KB):
                     nc.tensor.matmul(
@@ -125,14 +124,15 @@ def tile_sparseattention_b_kernel(tc, q, k, v, offs, out):
                     start=(jb == 0),
                     stop=(jb == KB - 1),
                 )
-            if half == PAIR - 1:
-                h, t = divmod(PAIR * w, BLOCKS)
-                o_sb = work.tile([P, PAIR * BQ], F32, name="o_sb")
-                if w % 2 == 0:
-                    nc.vector.tensor_copy(o_sb[:], o_ps[w][:])
-                else:
-                    nc.scalar.copy(o_sb[:], o_ps[w][:])
-                nc.sync.dma_start(out[h * P : (h + 1) * P, t * BQ : (t + PAIR) * BQ], o_sb[:])
+
+        def leave(w):
+            h, t = divmod(PAIR * w, BLOCKS)
+            o_sb = work.tile([P, PAIR * BQ], F32, name="o_sb")
+            if w % 2 == 0:
+                nc.vector.tensor_copy(o_sb[:], o_ps[w][:])
+            else:
+                nc.scalar.copy(o_sb[:], o_ps[w][:])
+            nc.sync.dma_start(out[h * P : (h + 1) * P, t * BQ : (t + PAIR) * BQ], o_sb[:])
 
         load_head(0)
         for u in range(3):
@@ -140,8 +140,10 @@ def tile_sparseattention_b_kernel(tc, q, k, v, offs, out):
         for u in range(2):
             for nb in range(QB):
                 score(u, nb)
-        for i in range(UNITS + 3):
-            if 0 <= i - 3:
+        for i in range(UNITS + 5):
+            if 0 <= i - 4 < UNITS and (i - 4) % PAIR == PAIR - 1:
+                leave((i - 4) // PAIR)
+            if 0 <= i - 3 < UNITS:
                 weigh(i - 3)
             if 0 <= i - 2 < UNITS:
                 flip_weights(i - 2)

@@ -77,6 +77,8 @@ def tile_sparseattention_b_kernel(tc, q, k, v, offs, out):
             n0 = t * BQ + nb * P
             s_ps[u, nb] = scores.tile([P, BK], F32, name="s_ps")
             nc.tensor.matmul(s_ps[u, nb][:], q_sb[h][:, n0 : n0 + P], keys[u][:], start=True, stop=True)
+
+        def top(u, nb):
             neg_max[u, nb] = stats.tile([P, 1], F32, name="neg_max")
             nc.vector.tensor_reduce(neg_max[u, nb][:], s_ps[u, nb][:], AXIS_X, MAX, negate=True)
 
@@ -140,11 +142,16 @@ def tile_sparseattention_b_kernel(tc, q, k, v, offs, out):
         for u in range(2):
             for nb in range(QB):
                 score(u, nb)
+        for nb in range(QB):
+            top(0, nb)
         for i in range(UNITS + 5):
             if 0 <= i - 4 < UNITS and (i - 4) % PAIR == PAIR - 1:
                 leave((i - 4) // PAIR)
             if 0 <= i - 3 < UNITS:
                 weigh(i - 3)
+            if i + 1 < UNITS:
+                for nb in range(QB):
+                    top(i + 1, nb)
             if 0 <= i - 2 < UNITS:
                 flip_weights(i - 2)
             if i + 3 < UNITS:

import concourse.mybir as mybir
from concourse.masks import make_identity

F32 = mybir.dt.float32
BF16 = mybir.dt.bfloat16
U16 = mybir.dt.uint16
COPY = mybir.ActivationFunctionType.Copy
EXP = mybir.ActivationFunctionType.Exp
MULT = mybir.AluOpType.mult
MAX = mybir.AluOpType.max
AXIS_X = mybir.AxisListType.X

P = 128
HEADS = 8
STORE = 4096
LIST = 2048
BLOCKS = 4
BQ = 256
BK = 512
NQ = BLOCKS * BQ
QB = BQ // P
KB = BK // P
UNITS = HEADS * BLOCKS
PAIR = 2
SM_SCALE = 0.125

FLOPS = 2 * 2 * HEADS * BLOCKS * BQ * BK * P


def tile_sparseattention_b_kernel(tc, q, k, v, offs, out):
    nc = tc.nc
    with (
        tc.tile_pool(name="held", bufs=1) as held,
        tc.tile_pool(name="store", bufs=3) as store,
        tc.tile_pool(name="heads", bufs=3) as heads,
        tc.tile_pool(name="work", bufs=12) as work,
        tc.tile_pool(name="stats", bufs=24) as stats,
        tc.psum_pool(name="scores", bufs=4) as scores,
        tc.psum_pool(name="flipped", bufs=2) as flipped,
        tc.psum_pool(name="products", bufs=2) as products,
    ):
        offsets = held.tile([P, LIST // 16], U16, name="offsets")
        nc.sync.dma_start(offsets[:], offs)
        ident = held.tile([P, P], BF16, name="ident")
        make_identity(nc, ident[:])
        warm = held.tile([P, 2], F32, name="warm")
        nc.vector.memset(warm[:], 0.0)
        nc.scalar.activation(warm[:, 1:2], warm[:, 0:1], EXP)

        k_win, q_sb, v_sb = {}, {}, {}
        keys, p_t = {}, {}
        v_t, o_ps = {}, {}
        s_ps, neg_max, p_sb = {}, {}, {}

        def load_head(h):
            rows = slice(h * P, (h + 1) * P)
            k_win[h] = store.tile([P, STORE], F32, name="k_win")
            nc.sync.dma_start(k_win[h][:], k[rows, :])
            q_sb[h] = heads.tile([P, NQ], BF16, name="q_sb")
            nc.sync.dma_start(q_sb[h][:], q[rows, :])
            v_sb[h] = heads.tile([P, LIST], BF16, name="v_sb")
            nc.sync.dma_start(v_sb[h][:], v[rows, :])

        def pick_keys(u):
            h, t = divmod(u, BLOCKS)
            if t == 0 and h + 1 < HEADS:
                load_head(h + 1)
            picked = work.tile([P, BK], F32, name="picked")
            piece = offsets[:, t * (BK // 16) : (t + 1) * (BK // 16)]
            nc.scalar.activation(picked[:], k_win[h][:].indirect(piece), COPY)
            keys[u] = work.tile([P, BK], BF16, name="keys")
            rounder = nc.vector if t % 2 == 0 else nc.gpsimd
            rounder.tensor_scalar(keys[u][:], picked[:], SM_SCALE, 1.0, MULT, MULT)

        def score(u, nb):
            h, t = divmod(u, BLOCKS)
            n0 = t * BQ + nb * P
            s_ps[u, nb] = scores.tile([P, BK], F32, name="s_ps")
            nc.tensor.matmul(s_ps[u, nb][:], q_sb[h][:, n0 : n0 + P], keys[u][:], start=True, stop=True)

        def top(u, nb):
            neg_max[u, nb] = stats.tile([P, 1], F32, name="neg_max")
            nc.vector.tensor_reduce(neg_max[u, nb][:], s_ps[u, nb][:], AXIS_X, MAX, negate=True)

        def flip_values(w):
            h, t = divmod(PAIR * w, BLOCKS)
            vt_ps = flipped.tile([P, PAIR * KB, P], BF16, name="vt_ps", tag="flipped")
            for jb in range(PAIR * KB):
                j0 = t * BK + jb * P
                nc.tensor.transpose(vt_ps[:, jb, :], v_sb[h][:, j0 : j0 + P], ident[:])
            v_t[w] = work.tile([P, PAIR * KB, P], BF16, name="v_t")
            nc.vector.tensor_copy(v_t[w][:], vt_ps[:])

        def soften(u, nb):
            e_sb = work.tile([P, BK], F32, name="e_sb")
            e_sum = stats.tile([P, 1], F32, name="e_sum")
            nc.scalar.activation(e_sb[:], s_ps[u, nb][:], EXP, bias=neg_max[u, nb][:], accum_out=e_sum[:])
            r_sum = stats.tile([P, 1], F32, name="r_sum")
            nc.vector.reciprocal(r_sum[:], e_sum[:])
            p_sb[u, nb] = work.tile([P, BK], BF16, name="p_sb")
            nc.gpsimd.tensor_scalar(p_sb[u, nb][:], e_sb[:], r_sum[:], 1.0, MULT, MULT)

        def flip_weights(u):
            pt_ps = flipped.tile([P, KB, BQ], BF16, name="pt_ps", tag="flipped")
            for nb in range(QB):
                for jb in range(KB):
                    nc.tensor.matmul(
                        pt_ps[:, jb, nb * P : (nb + 1) * P],
                        p_sb[u, nb][:, jb * P : (jb + 1) * P],
                        ident[:],
                        start=True,
                        stop=True,
                    )
            p_t[u] = work.tile([P, KB, BQ], BF16, name="p_t")
            nc.vector.tensor_copy(p_t[u][:], pt_ps[:])

        def weigh(u):
            w, half = divmod(u, PAIR)
            if half == 0:
                o_ps[w] = products.tile([P, PAIR * BQ], F32, name="o_ps")
            for jb in range(KB):
                nc.tensor.matmul(
                    o_ps[w][:, half * BQ : (half + 1) * BQ],
                    v_t[w][:, half * KB + jb, :],
                    p_t[u][:, jb, :],
                    start=(jb == 0),
                    stop=(jb == KB - 1),
                )

        def leave(w):
            h, t = divmod(PAIR * w, BLOCKS)
            o_sb = work.tile([P, PAIR * BQ], F32, name="o_sb")
            if w % 2 == 0:
                nc.vector.tensor_copy(o_sb[:], o_ps[w][:])
            else:
                nc.scalar.copy(o_sb[:], o_ps[w][:])
            nc.sync.dma_start(out[h * P : (h + 1) * P, t * BQ : (t + PAIR) * BQ], o_sb[:])

        load_head(0)
        for u in range(3):
            pick_keys(u)
        for u in range(2):
            for nb in range(QB):
                score(u, nb)
        for nb in range(QB):
            top(0, nb)
        for i in range(UNITS + 5):
            if 0 <= i - 4 < UNITS and (i - 4) % PAIR == PAIR - 1:
                leave((i - 4) // PAIR)
            if 0 <= i - 3 < UNITS:
                weigh(i - 3)
            if i + 1 < UNITS:
                for nb in range(QB):
                    top(i + 1, nb)
            if 0 <= i - 2 < UNITS:
                flip_weights(i - 2)
            if i + 3 < UNITS:
                pick_keys(i + 3)
            if i < UNITS:
                for nb in range(QB):
                    soften(i, nb)
                    if i + 2 < UNITS:
                        score(i + 2, nb)
                if i % PAIR == 0:
                    flip_values(i // PAIR)
